import numpy as np
import ml_dtypes


def mxq(x, axis, fmt="e4m3"):
    dtype, down = {"e4m3": (ml_dtypes.float8_e4m3fn, 7), "e5m2": (ml_dtypes.float8_e5m2, 14)}[fmt]
    v = np.moveaxis(np.asarray(x, np.float32).astype(ml_dtypes.bfloat16).astype(np.float64), axis, -1)
    blocks = v.reshape(v.shape[:-1] + (-1, 32))
    amax = np.abs(blocks).max(-1, keepdims=True)
    byte = np.maximum(np.where(amax > 0, np.frexp(amax)[1] - 1 + 127, 0) - down, 1)
    scale = np.exp2(byte - 127.0)
    codes = (blocks / scale).astype(np.float32).astype(dtype).astype(np.float64)
    return np.moveaxis((codes * scale).reshape(v.shape), -1, axis)


WIDE = False


def mx_kscale(k):
    if not WIDE:
        return np.ones(k)
    levels = np.array([10, -10, 5, -5, 0])
    a = np.random.permutation(np.resize(levels, k // 512 * 4)).reshape(k // 512, 4)
    idx = np.arange(k)
    return np.exp2(a[idx // 512, idx % 128 // 32])


BF16 = ml_dtypes.bfloat16


def bf(x):
    return np.asarray(x, np.float32).astype(BF16)


def f64(x):
    return np.asarray(x).astype(np.float64)


E2M1 = np.array([0.0, 0.5, 1.0, 1.5, 2.0, 3.0, 4.0, 6.0, -0.0, -0.5, -1.0, -1.5, -2.0, -3.0, -4.0, -6.0])


def pack_weight(w, fmt):
    k, n = w.shape
    w = f64(bf(w)).reshape(k // 32, 32, n)
    amax = np.abs(w).max(1)
    if fmt == "e4m3":
        byte = np.frexp(amax)[1] - 1 + 127 - 7
    else:
        mant, ex = np.frexp(amax / 6.0)
        byte = np.where(mant > 0.5, ex, ex - 1) + 127
    byte = np.clip(np.where(amax > 0, byte, 1), 1, 254)
    scaled = (w * np.exp2(127.0 - byte)[:, None, :]).reshape(k, n).astype(np.float32)
    by_word = np.ascontiguousarray(scaled.reshape(k // 512, 128, 4, n).transpose(0, 1, 3, 2))
    if fmt == "e4m3":
        words = by_word.astype(ml_dtypes.float8_e4m3fn).view(np.uint8)
    else:
        c = by_word.astype(ml_dtypes.float4_e2m1fn).view(np.uint8) & 0xF
        words = c[..., 0::2] | (c[..., 1::2] << 4)
    return np.ascontiguousarray(words), np.ascontiguousarray(byte.astype(np.uint8).reshape(k // 512, 16, n))


def unpack_weight(words, scales, fmt):
    g, p, n, _ = words.shape
    if fmt == "e4m3":
        vals = np.ascontiguousarray(words).view(ml_dtypes.float8_e4m3fn).astype(np.float64)
    else:
        nib = np.empty((g, p, n, 4), np.uint8)
        nib[..., 0::2] = words & 0xF
        nib[..., 1::2] = words >> 4
        vals = E2M1[nib]
    vals = vals * np.repeat(np.exp2(scales.astype(np.float64) - 127.0), 8, axis=1)[..., None]
    return vals.transpose(0, 1, 3, 2).reshape(g * 512, n)

def pack4(w):
    words, scales = pack_weight(w, "e2m1")
    return words.reshape(words.shape[0], 128, -1), scales


def unpack4(words, scales):
    return unpack_weight(words.reshape(words.shape[0], 128, -1, 2), scales, "e2m1")


B, S, HID, H, HKV, DH = 2, 128, 2048, 16, 16, 128
NH = H + 2 * HKV


def rotate_half(x):
    x1 = x[..., ::2]
    x2 = x[..., 1::2]
    return np.stack((-x2, x1), axis=-1).reshape(x.shape)


def setup_inputs():
    s = mx_kscale(HID)
    inv_freq = 1.0 / (10000.0 ** (np.arange(0, DH, 2) / DH))
    emb = np.repeat(np.outer(np.arange(S), inv_freq), 2, axis=-1)
    hidden_states = bf(np.random.standard_normal((B, S, HID)) * s)
    cos = bf(np.cos(emb))
    sin = bf(np.sin(emb))
    w = np.random.standard_normal((NH * DH, HID)) / np.sqrt(HID) / s[None, :]
    words, scales = pack4(np.ascontiguousarray(w.T))
    return {"hidden_states": hidden_states,
            "cos": cos,
            "sin": sin,
            "w_qkv_words": words,
            "w_qkv_scales": scales}


def reference(hidden_states, cos, sin, w_qkv_words, w_qkv_scales):
    qkv = mxq(f64(hidden_states), 2, "e4m3") @ unpack4(w_qkv_words, w_qkv_scales)
    qkv = qkv.reshape(B, S, NH, DH)
    q = qkv[:, :, :H]
    k = qkv[:, :, H:H + HKV]
    v = qkv[:, :, H + HKV:]
    cos_s = f64(cos)[:S][None, :, None, :]
    sin_s = f64(sin)[:S][None, :, None, :]
    q = q * cos_s + rotate_half(q) * sin_s
    k = k * cos_s + rotate_half(k) * sin_s
    return q, k, v

@@ -1,0 +1,158 @@
+from contextlib import ExitStack
+
+import concourse.mybir as mybir
+from concourse.masks import make_identity
+
+F32 = mybir.dt.float32
+BF16 = mybir.dt.bfloat16
+I32 = mybir.dt.int32
+U32 = mybir.dt.uint32
+U8 = mybir.dt.uint8
+FP8X4 = mybir.dt.float8_e4m3fn_x4
+FP4X4 = mybir.dt.float4_e2m1fn_x4
+MULT = mybir.AluOpType.mult
+ADD = mybir.AluOpType.add
+
+P = 128
+BATCHES = 2
+HID = 2048
+K_PASS = 4 * P
+PASSES = HID // K_PASS
+PARTS = 3
+FEATURES = 2048
+BANK = 512
+CHUNK = 1024
+ROUNDS = FEATURES // CHUNK
+HEADS_IN_BANK = BANK // P
+HEADS_IN_CHUNK = CHUNK // P
+PAIRS = P // 2
+BANK_PAIRS = BANK // 2
+
+FLOPS = 2 * BATCHES * P * HID * PARTS * FEATURES
+
+
+def tile_attention_pa_kernel(
+    tc, hidden_states, cos, sin, w_qkv_words, w_qkv_scales, out_0, out_1, out_2
+):
+    nc = tc.nc
+    outs = (out_0, out_1, out_2)
+
+    with ExitStack() as stack:
+        keep = stack.enter_context(tc.tile_pool(name="keep", bufs=1))
+        stage = stack.enter_context(tc.tile_pool(name="stage", bufs=4))
+        psum = stack.enter_context(tc.psum_pool(name="psum", bufs=8))
+
+        x_rows = []
+        for b in range(BATCHES):
+            x_sb = keep.tile([P, HID], BF16, name="x_rows_%d" % b)
+            nc.sync.dma_start(out=x_sb[:], in_=hidden_states[b])
+            x_rows.append(x_sb)
+        cos_sb = keep.tile([P, P], BF16, name="cos_sb")
+        nc.sync.dma_start(out=cos_sb[:], in_=cos)
+        sin_sb = keep.tile([P, P], BF16, name="sin_sb")
+        nc.sync.dma_start(out=sin_sb[:], in_=sin)
+
+        w_words = {}
+        w_scales = {}
+        for r in range(ROUNDS):
+            for part in range(PARTS):
+                first = part * FEATURES + r * CHUNK
+                scales = keep.tile([P, PASSES, CHUNK], U8, name="w_scales_%d_%d" % (part, r), align_bytes=64)
+                nc.vector.memset(scales[:].bitcast(I32), 0)
+                for q in range(8):
+                    nc.sync.dma_start(
+                        out=scales[32 * (q // 4) + q % 4 : P : 64].bitcast(I32),
+                        in_=w_qkv_scales[:, q : 16 : 8, first : first + CHUNK]
+                        .bitcast(I32)
+                        .rearrange("g j c -> j g c"),
+                    )
+                words = keep.tile([P, PASSES, 2 * CHUNK], U8, name="w_words_%d_%d" % (part, r), align_bytes=64)
+                nc.sync.dma_start(
+                    out=words[:].bitcast(I32),
+                    in_=w_qkv_words[:, :, 2 * first : 2 * (first + CHUNK)]
+                    .bitcast(I32)
+                    .rearrange("g p c -> p g c"),
+                )
+                w_words[(part, r)] = words
+                w_scales[(part, r)] = scales
+
+        cos_lanes = cos_sb[:].rearrange("p (i e) -> p e i", e=2)
+        sin_lanes = sin_sb[:].rearrange("p (i e) -> p e i", e=2)
+        factors = keep.tile([P, 2, 2, PAIRS], F32, name="factors")
+        nc.vector.tensor_copy(out=factors[:, 0, 0, :], in_=cos_lanes[:, 0, :])
+        nc.vector.tensor_copy(out=factors[:, 0, 1, :], in_=sin_lanes[:, 1, :])
+        nc.vector.tensor_scalar_mul(out=factors[:, 1, 0, :], in0=sin_lanes[:, 0, :], scalar1=-1.0)
+        nc.vector.tensor_copy(out=factors[:, 1, 1, :], in_=cos_lanes[:, 1, :])
+
+        identity = keep.tile([P, P], F32, name="identity")
+        make_identity(nc, identity[:])
+        x_codes = keep.tile([P, BATCHES, PASSES, P], U32, name="x_codes", align_bytes=64)
+        x_scales = keep.tile([P, BATCHES, PASSES, P], U8, name="x_scales", align_bytes=64)
+        for b in range(BATCHES):
+            x_words = x_rows[b][:].bitcast(F32)
+            for half in range(PASSES // 2):
+                turned = psum.tile([P, 2, 2, P], F32, tag="bank")
+                for gi in range(2):
+                    g = 2 * half + gi
+                    for u in range(2):
+                        nc.tensor.transpose(
+                            turned[:, gi, u, :],
+                            x_words[:, 256 * g + u : 256 * (g + 1) : 2],
+                            identity[:],
+                        )
+                grouped = stage.tile([P, 2, P, 4], BF16, align_bytes=64)
+                copy_out = nc.vector.tensor_copy if half == 0 else nc.scalar.copy
+                copy_out(out=grouped[:].bitcast(F32), in_=turned[:].rearrange("p g u r -> p g r u"))
+                passes = slice(2 * half, 2 * half + 2)
+                nc.vector.quantize_mx(
+                    out=x_codes[:, b, passes, :].rearrange("p g r -> p (g r)").bitcast(FP8X4),
+                    scales=x_scales[:, b, passes, :].rearrange("p g r -> p (g r)"),
+                    in_=grouped[:].rearrange("p g r t -> p (g r t)"),
+                )
+
+        for r in range(ROUNDS):
+            for part in range(PARTS):
+                words = w_words[(part, r)]
+                scales = w_scales[(part, r)]
+                for b in range(BATCHES):
+                    result = keep.tile([P, CHUNK], F32, name="result_%d_%d_%d" % (part, r, b))
+                    for c in range(CHUNK // BANK):
+                        acc = psum.tile([P, BANK], F32, tag="bank")
+                        for g in range(PASSES):
+                            nc.tensor.matmul_mx(
+                                out=acc[:],
+                                lhsT=x_codes[:, b, g, :].bitcast(FP8X4),
+                                lhsT_scale=x_scales[:, b, g, :],
+                                rhs=words[:, g, 2 * BANK * c : 2 * BANK * (c + 1)].bitcast(FP4X4),
+                                rhs_scale=scales[:, g, BANK * c : BANK * (c + 1)],
+                                start=(g == 0),
+                                stop=(g == PASSES - 1),
+                            )
+                        dest = result[:, BANK * c : BANK * (c + 1)]
+                        if part == PARTS - 1:
+                            nc.scalar.copy(out=dest, in_=acc[:])
+                        else:
+                            lanes = acc[:].rearrange("p (n e) -> p e n", e=2)
+                            products = stage.tile([P, 4, BANK_PAIRS], F32)
+                            for e in range(2):
+                                nc.vector.tensor_tensor(
+                                    out=products[:, 2 * e : 2 * e + 2, :].rearrange("p t (h i) -> p t h i", i=PAIRS),
+                                    in0=lanes[:, e : e + 1, :]
+                                    .to_broadcast([P, 2, BANK_PAIRS])
+                                    .rearrange("p t (h i) -> p t h i", i=PAIRS),
+                                    in1=factors[:, e, :, :]
+                                    .unsqueeze(2)
+                                    .to_broadcast([P, 2, HEADS_IN_BANK, PAIRS]),
+                                    op=MULT,
+                                )
+                            nc.gpsimd.tensor_tensor(
+                                out=dest.rearrange("p (n e) -> p n e", e=2),
+                                in0=products[:, 0:2, :].rearrange("p e n -> p n e"),
+                                in1=products[:, 2:4, :].rearrange("p e n -> p n e"),
+                                op=ADD,
+                            )
+                    heads = slice(HEADS_IN_CHUNK * r, HEADS_IN_CHUNK * (r + 1))
+                    nc.sync.dma_start(
+                        out=outs[part][b, :, heads, :].rearrange("s h d -> s (h d)"),
+                        in_=result[:],
+                    )

@@ -38,6 +38,7 @@ def tile_attention_pa_kernel(
     outs = (out_0, out_1, out_2)
 
     with ExitStack() as stack:
+        stack.enter_context(tc.manual_schedule())
         keep = stack.enter_context(tc.tile_pool(name="keep", bufs=1))
         stage = stack.enter_context(tc.tile_pool(name="stage", bufs=4))
         psum = stack.enter_context(tc.psum_pool(name="psum", bufs=8))
@@ -56,16 +57,18 @@ def tile_attention_pa_kernel(
         w_scales = {}
         for r in range(ROUNDS):
             for part in range(PARTS):
+                if r == 0:
+                    scales = keep.tile([P, PASSES, FEATURES], U8, name="w_scales_%d" % part, align_bytes=64)
+                    nc.vector.memset(scales[:].bitcast(I32), 0)
+                    for q in range(8):
+                        nc.sync.dma_start(
+                            out=scales[32 * (q // 4) + q % 4 : P : 64].bitcast(I32),
+                            in_=w_qkv_scales[:, q : 16 : 8, part * FEATURES : (part + 1) * FEATURES]
+                            .bitcast(I32)
+                            .rearrange("g j c -> j g c"),
+                        )
+                    w_scales[part] = scales
                 first = part * FEATURES + r * CHUNK
-                scales = keep.tile([P, PASSES, CHUNK], U8, name="w_scales_%d_%d" % (part, r), align_bytes=64)
-                nc.vector.memset(scales[:].bitcast(I32), 0)
-                for q in range(8):
-                    nc.sync.dma_start(
-                        out=scales[32 * (q // 4) + q % 4 : P : 64].bitcast(I32),
-                        in_=w_qkv_scales[:, q : 16 : 8, first : first + CHUNK]
-                        .bitcast(I32)
-                        .rearrange("g j c -> j g c"),
-                    )
                 words = keep.tile([P, PASSES, 2 * CHUNK], U8, name="w_words_%d_%d" % (part, r), align_bytes=64)
                 nc.sync.dma_start(
                     out=words[:].bitcast(I32),
@@ -74,15 +77,6 @@ def tile_attention_pa_kernel(
                     .rearrange("g p c -> p g c"),
                 )
                 w_words[(part, r)] = words
-                w_scales[(part, r)] = scales
-
-        cos_lanes = cos_sb[:].rearrange("p (i e) -> p e i", e=2)
-        sin_lanes = sin_sb[:].rearrange("p (i e) -> p e i", e=2)
-        factors = keep.tile([P, 2, 2, PAIRS], F32, name="factors")
-        nc.vector.tensor_copy(out=factors[:, 0, 0, :], in_=cos_lanes[:, 0, :])
-        nc.vector.tensor_copy(out=factors[:, 0, 1, :], in_=sin_lanes[:, 1, :])
-        nc.vector.tensor_scalar_mul(out=factors[:, 1, 0, :], in0=sin_lanes[:, 0, :], scalar1=-1.0)
-        nc.vector.tensor_copy(out=factors[:, 1, 1, :], in_=cos_lanes[:, 1, :])
 
         identity = keep.tile([P, P], F32, name="identity")
         make_identity(nc, identity[:])
@@ -110,10 +104,18 @@ def tile_attention_pa_kernel(
                     in_=grouped[:].rearrange("p g r t -> p (g r t)"),
                 )
 
+        cos_lanes = cos_sb[:].rearrange("p (i e) -> p e i", e=2)
+        sin_lanes = sin_sb[:].rearrange("p (i e) -> p e i", e=2)
+        factors = keep.tile([P, 2, 2, PAIRS], F32, name="factors")
+        nc.vector.tensor_copy(out=factors[:, 0, 0, :], in_=cos_lanes[:, 0, :])
+        nc.vector.tensor_copy(out=factors[:, 0, 1, :], in_=sin_lanes[:, 1, :])
+        nc.vector.tensor_scalar_mul(out=factors[:, 1, 0, :], in0=sin_lanes[:, 0, :], scalar1=-1.0)
+        nc.vector.tensor_copy(out=factors[:, 1, 1, :], in_=cos_lanes[:, 1, :])
+
         for r in range(ROUNDS):
             for part in range(PARTS):
                 words = w_words[(part, r)]
-                scales = w_scales[(part, r)]
+                scales = w_scales[part]
                 for b in range(BATCHES):
                     result = keep.tile([P, CHUNK], F32, name="result_%d_%d_%d" % (part, r, b))
                     for c in range(CHUNK // BANK):
@@ -124,7 +126,7 @@ def tile_attention_pa_kernel(
                                 lhsT=x_codes[:, b, g, :].bitcast(FP8X4),
                                 lhsT_scale=x_scales[:, b, g, :],
                                 rhs=words[:, g, 2 * BANK * c : 2 * BANK * (c + 1)].bitcast(FP4X4),
-                                rhs_scale=scales[:, g, BANK * c : BANK * (c + 1)],
+                                rhs_scale=scales[:, g, CHUNK * r + BANK * c : CHUNK * r + BANK * (c + 1)],
                                 start=(g == 0),
                                 stop=(g == PASSES - 1),
                             )
@@ -145,7 +147,8 @@ def tile_attention_pa_kernel(
                                     .to_broadcast([P, 2, HEADS_IN_BANK, PAIRS]),
                                     op=MULT,
                                 )
-                            nc.gpsimd.tensor_tensor(
+                            adder = nc.vector if (b == BATCHES - 1 and c == CHUNK // BANK - 1) else nc.gpsimd
+                            adder.tensor_tensor(
                                 out=dest.rearrange("p (n e) -> p n e", e=2),
                                 in0=products[:, 0:2, :].rearrange("p e n -> p n e"),
                                 in1=products[:, 2:4, :].rearrange("p e n -> p n e"),

@@ -19,14 +19,12 @@ HID = 2048
 K_PASS = 4 * P
 PASSES = HID // K_PASS
 PARTS = 3
+V_PART = 2
 FEATURES = 2048
 BANK = 512
-CHUNK = 1024
-ROUNDS = FEATURES // CHUNK
+BANKS = FEATURES // BANK
 HEADS_IN_BANK = BANK // P
-HEADS_IN_CHUNK = CHUNK // P
 PAIRS = P // 2
-BANK_PAIRS = BANK // 2
 
 FLOPS = 2 * BATCHES * P * HID * PARTS * FEATURES
 
@@ -53,30 +51,33 @@ def tile_attention_pa_kernel(
         sin_sb = keep.tile([P, P], BF16, name="sin_sb")
         nc.sync.dma_start(out=sin_sb[:], in_=sin)
 
-        w_words = {}
-        w_scales = {}
-        for r in range(ROUNDS):
-            for part in range(PARTS):
-                if r == 0:
-                    scales = keep.tile([P, PASSES, FEATURES], U8, name="w_scales_%d" % part, align_bytes=64)
-                    nc.vector.memset(scales[:].bitcast(I32), 0)
-                    for q in range(8):
-                        nc.sync.dma_start(
-                            out=scales[32 * (q // 4) + q % 4 : P : 64].bitcast(I32),
-                            in_=w_qkv_scales[:, q : 16 : 8, part * FEATURES : (part + 1) * FEATURES]
-                            .bitcast(I32)
-                            .rearrange("g j c -> j g c"),
-                        )
-                    w_scales[part] = scales
-                first = part * FEATURES + r * CHUNK
-                words = keep.tile([P, PASSES, 2 * CHUNK], U8, name="w_words_%d_%d" % (part, r), align_bytes=64)
+        w_scales = []
+        w_words = []
+        for part in range(PARTS):
+            scales = keep.tile([P, PASSES, FEATURES], U8, name="w_scales_%d" % part, align_bytes=64)
+            nc.vector.memset(scales[:].bitcast(I32), 0)
+            for q in range(8):
+                nc.sync.dma_start(
+                    out=scales[32 * (q // 4) + q % 4 : P : 64].bitcast(I32),
+                    in_=w_qkv_scales[:, q : 16 : 8, part * FEATURES : (part + 1) * FEATURES]
+                    .bitcast(I32)
+                    .rearrange("g j c -> j g c"),
+                )
+            w_scales.append(scales)
+            pieces = 2 if part == 0 else 1
+            width = FEATURES // pieces
+            tiles = []
+            for i in range(pieces):
+                first = part * FEATURES + i * width
+                words = keep.tile([P, PASSES, 2 * width], U8, name="w_words_%d_%d" % (part, i), align_bytes=64)
                 nc.sync.dma_start(
                     out=words[:].bitcast(I32),
-                    in_=w_qkv_words[:, :, 2 * first : 2 * (first + CHUNK)]
+                    in_=w_qkv_words[:, :, 2 * first : 2 * (first + width)]
                     .bitcast(I32)
                     .rearrange("g p c -> p g c"),
                 )
-                w_words[(part, r)] = words
+                tiles.append(words)
+            w_words.append(tiles)
 
         identity = keep.tile([P, P], F32, name="identity")
         make_identity(nc, identity[:])
@@ -104,58 +105,55 @@ def tile_attention_pa_kernel(
                     in_=grouped[:].rearrange("p g r t -> p (g r t)"),
                 )
 
-        cos_lanes = cos_sb[:].rearrange("p (i e) -> p e i", e=2)
-        sin_lanes = sin_sb[:].rearrange("p (i e) -> p e i", e=2)
-        factors = keep.tile([P, 2, 2, PAIRS], F32, name="factors")
-        nc.vector.tensor_copy(out=factors[:, 0, 0, :], in_=cos_lanes[:, 0, :])
-        nc.vector.tensor_copy(out=factors[:, 0, 1, :], in_=sin_lanes[:, 1, :])
-        nc.vector.tensor_scalar_mul(out=factors[:, 1, 0, :], in0=sin_lanes[:, 0, :], scalar1=-1.0)
-        nc.vector.tensor_copy(out=factors[:, 1, 1, :], in_=cos_lanes[:, 1, :])
+        cos_pairs = cos_sb[:].rearrange("p (i t) -> p i t", t=2)
+        sin_pairs = sin_sb[:].rearrange("p (i t) -> p i t", t=2)
+        factors = keep.tile([P, 2, PAIRS, 2], F32, name="factors")
+        nc.vector.tensor_copy(out=factors[:, 0, :, 0], in_=cos_pairs[:, :, 0])
+        nc.vector.tensor_copy(out=factors[:, 0, :, 1], in_=sin_pairs[:, :, 1])
+        nc.vector.tensor_scalar_mul(out=factors[:, 1, :, 0], in0=sin_pairs[:, :, 0], scalar1=-1.0)
+        nc.vector.tensor_copy(out=factors[:, 1, :, 1], in_=cos_pairs[:, :, 1])
+        rotation_shape = [P, 2, HEADS_IN_BANK, PAIRS, 2]
 
-        for r in range(ROUNDS):
-            for part in range(PARTS):
-                words = w_words[(part, r)]
-                scales = w_scales[part]
-                for b in range(BATCHES):
-                    result = keep.tile([P, CHUNK], F32, name="result_%d_%d_%d" % (part, r, b))
-                    for c in range(CHUNK // BANK):
-                        acc = psum.tile([P, BANK], F32, tag="bank")
-                        for g in range(PASSES):
-                            nc.tensor.matmul_mx(
-                                out=acc[:],
-                                lhsT=x_codes[:, b, g, :].bitcast(FP8X4),
-                                lhsT_scale=x_scales[:, b, g, :],
-                                rhs=words[:, g, 2 * BANK * c : 2 * BANK * (c + 1)].bitcast(FP4X4),
-                                rhs_scale=scales[:, g, CHUNK * r + BANK * c : CHUNK * r + BANK * (c + 1)],
-                                start=(g == 0),
-                                stop=(g == PASSES - 1),
-                            )
-                        dest = result[:, BANK * c : BANK * (c + 1)]
-                        if part == PARTS - 1:
-                            nc.scalar.copy(out=dest, in_=acc[:])
-                        else:
-                            lanes = acc[:].rearrange("p (n e) -> p e n", e=2)
-                            products = stage.tile([P, 4, BANK_PAIRS], F32)
-                            for e in range(2):
-                                nc.vector.tensor_tensor(
-                                    out=products[:, 2 * e : 2 * e + 2, :].rearrange("p t (h i) -> p t h i", i=PAIRS),
-                                    in0=lanes[:, e : e + 1, :]
-                                    .to_broadcast([P, 2, BANK_PAIRS])
-                                    .rearrange("p t (h i) -> p t h i", i=PAIRS),
-                                    in1=factors[:, e, :, :]
-                                    .unsqueeze(2)
-                                    .to_broadcast([P, 2, HEADS_IN_BANK, PAIRS]),
-                                    op=MULT,
-                                )
-                            adder = nc.vector if (b == BATCHES - 1 and c == CHUNK // BANK - 1) else nc.gpsimd
-                            adder.tensor_tensor(
-                                out=dest.rearrange("p (n e) -> p n e", e=2),
-                                in0=products[:, 0:2, :].rearrange("p e n -> p n e"),
-                                in1=products[:, 2:4, :].rearrange("p e n -> p n e"),
-                                op=ADD,
-                            )
-                    heads = slice(HEADS_IN_CHUNK * r, HEADS_IN_CHUNK * (r + 1))
-                    nc.sync.dma_start(
-                        out=outs[part][b, :, heads, :].rearrange("s h d -> s (h d)"),
-                        in_=result[:],
-                    )
+        for part in range(PARTS):
+            banks_in_tile = BANKS // len(w_words[part])
+            banks_in_store = 1 if part == V_PART else 2
+            for b in range(BATCHES):
+                result = keep.tile([P, FEATURES], F32, name="result_%d_%d" % (part, b))
+                for j in range(BANKS):
+                    words = w_words[part][j // banks_in_tile]
+                    at = BANK * (j % banks_in_tile)
+                    acc = psum.tile([P, BANK], F32, tag="bank")
+                    for g in range(PASSES):
+                        nc.tensor.matmul_mx(
+                            out=acc[:],
+                            lhsT=x_codes[:, b, g, :].bitcast(FP8X4),
+                            lhsT_scale=x_scales[:, b, g, :],
+                            rhs=words[:, g, 2 * at : 2 * (at + BANK)].bitcast(FP4X4),
+                            rhs_scale=w_scales[part][:, g, BANK * j : BANK * (j + 1)],
+                            start=(g == 0),
+                            stop=(g == PASSES - 1),
+                        )
+                    dest = result[:, BANK * j : BANK * (j + 1)]
+                    if part == V_PART:
+                        nc.scalar.copy(out=dest, in_=acc[:])
+                    else:
+                        products = stage.tile([P, 2, BANK], F32)
+                        nc.vector.tensor_tensor(
+                            out=products[:].rearrange("p e (h i t) -> p e h i t", i=PAIRS, t=2),
+                            in0=acc[:]
+                            .rearrange("p (h i e) -> p e h i", i=PAIRS, e=2)
+                            .unsqueeze(4)
+                            .to_broadcast(rotation_shape),
+                            in1=factors[:].unsqueeze(2).to_broadcast(rotation_shape),
+                            op=MULT,
+                        )
+                        adder = nc.vector if j == BANKS - 1 else nc.gpsimd
+                        adder.tensor_tensor(out=dest, in0=products[:, 0, :], in1=products[:, 1, :], op=ADD)
+                    if (j + 1) % banks_in_store == 0:
+                        j0 = j + 1 - banks_in_store
+                        nc.sync.dma_start(
+                            out=outs[part][b, :, HEADS_IN_BANK * j0 : HEADS_IN_BANK * (j + 1), :].rearrange(
+                                "s h d -> s (h d)"
+                            ),
+                            in_=result[:, BANK * j0 : BANK * (j + 1)],
+                        )

@@ -25,6 +25,7 @@ BANK = 512
 BANKS = FEATURES // BANK
 HEADS_IN_BANK = BANK // P
 PAIRS = P // 2
+CHUNKS = (512, 512, 1024, 1024, 1024, 1024, 1024)
 
 FLOPS = 2 * BATCHES * P * HID * PARTS * FEATURES
 
@@ -47,37 +48,34 @@ def tile_attention_pa_kernel(
             nc.sync.dma_start(out=x_sb[:], in_=hidden_states[b])
             x_rows.append(x_sb)
         cos_sb = keep.tile([P, P], BF16, name="cos_sb")
-        nc.sync.dma_start(out=cos_sb[:], in_=cos)
         sin_sb = keep.tile([P, P], BF16, name="sin_sb")
-        nc.sync.dma_start(out=sin_sb[:], in_=sin)
 
         w_scales = []
         w_words = []
-        for part in range(PARTS):
-            scales = keep.tile([P, PASSES, FEATURES], U8, name="w_scales_%d" % part, align_bytes=64)
+        first = 0
+        for c, width in enumerate(CHUNKS):
+            scales = keep.tile([P, PASSES, width], U8, name="w_scales_%d" % c, align_bytes=64)
             nc.vector.memset(scales[:].bitcast(I32), 0)
-            for q in range(8):
+            for r in range(4):
                 nc.sync.dma_start(
-                    out=scales[32 * (q // 4) + q % 4 : P : 64].bitcast(I32),
-                    in_=w_qkv_scales[:, q : 16 : 8, part * FEATURES : (part + 1) * FEATURES]
+                    out=scales[r : P : 32].bitcast(I32),
+                    in_=w_qkv_scales[:, r : 16 : 4, first : first + width]
                     .bitcast(I32)
                     .rearrange("g j c -> j g c"),
                 )
             w_scales.append(scales)
-            pieces = 2 if part == 0 else 1
-            width = FEATURES // pieces
-            tiles = []
-            for i in range(pieces):
-                first = part * FEATURES + i * width
-                words = keep.tile([P, PASSES, 2 * width], U8, name="w_words_%d_%d" % (part, i), align_bytes=64)
-                nc.sync.dma_start(
-                    out=words[:].bitcast(I32),
-                    in_=w_qkv_words[:, :, 2 * first : 2 * (first + width)]
-                    .bitcast(I32)
-                    .rearrange("g p c -> p g c"),
-                )
-                tiles.append(words)
-            w_words.append(tiles)
+            words = keep.tile([P, PASSES, 2 * width], U8, name="w_words_%d" % c, align_bytes=64)
+            nc.sync.dma_start(
+                out=words[:].bitcast(I32),
+                in_=w_qkv_words[:, :, 2 * first : 2 * (first + width)]
+                .bitcast(I32)
+                .rearrange("g p c -> p g c"),
+            )
+            w_words.append(words)
+            first += width
+            if c == 0:
+                nc.sync.dma_start(out=cos_sb[:], in_=cos)
+                nc.sync.dma_start(out=sin_sb[:], in_=sin)
 
         identity = keep.tile([P, P], F32, name="identity")
         make_identity(nc, identity[:])
@@ -114,22 +112,26 @@ def tile_attention_pa_kernel(
         nc.vector.tensor_copy(out=factors[:, 1, :, 1], in_=cos_pairs[:, :, 1])
         rotation_shape = [P, 2, HEADS_IN_BANK, PAIRS, 2]
 
-        for part in range(PARTS):
-            banks_in_tile = BANKS // len(w_words[part])
+        results = {}
+        first = 0
+        for c, width in enumerate(CHUNKS):
+            part = first // FEATURES
             banks_in_store = 1 if part == V_PART else 2
             for b in range(BATCHES):
-                result = keep.tile([P, FEATURES], F32, name="result_%d_%d" % (part, b))
-                for j in range(BANKS):
-                    words = w_words[part][j // banks_in_tile]
-                    at = BANK * (j % banks_in_tile)
+                if (part, b) not in results:
+                    results[(part, b)] = keep.tile([P, FEATURES], F32, name="result_%d_%d" % (part, b))
+                result = results[(part, b)]
+                for i in range(width // BANK):
+                    j = (first % FEATURES) // BANK + i
+                    at = BANK * i
                     acc = psum.tile([P, BANK], F32, tag="bank")
                     for g in range(PASSES):
                         nc.tensor.matmul_mx(
                             out=acc[:],
                             lhsT=x_codes[:, b, g, :].bitcast(FP8X4),
                             lhsT_scale=x_scales[:, b, g, :],
-                            rhs=words[:, g, 2 * at : 2 * (at + BANK)].bitcast(FP4X4),
-                            rhs_scale=w_scales[part][:, g, BANK * j : BANK * (j + 1)],
+                            rhs=w_words[c][:, g, 2 * at : 2 * (at + BANK)].bitcast(FP4X4),
+                            rhs_scale=w_scales[c][:, g, at : at + BANK],
                             start=(g == 0),
                             stop=(g == PASSES - 1),
                         )
@@ -157,3 +159,4 @@ def tile_attention_pa_kernel(
                             ),
                             in_=result[:, BANK * j0 : BANK * (j + 1)],
                         )
+            first += width

@@ -26,6 +26,8 @@ BANKS = FEATURES // BANK
 HEADS_IN_BANK = BANK // P
 PAIRS = P // 2
 CHUNKS = (512, 512, 1024, 1024, 1024, 1024, 1024)
+WARM_FIRST = 6
+WARM_BETWEEN = 1
 
 FLOPS = 2 * BATCHES * P * HID * PARTS * FEATURES
 
@@ -42,18 +44,34 @@ def tile_attention_pa_kernel(
         stage = stack.enter_context(tc.tile_pool(name="stage", bufs=4))
         psum = stack.enter_context(tc.psum_pool(name="psum", bufs=8))
 
+        zeros = keep.tile([P, BANK], BF16, name="zeros")
+        nc.vector.memset(zeros[:], 0.0)
+        table_warm = keep.tile([P, 1], BF16, name="table_warm")
+        nc.scalar.copy(out=table_warm[:], in_=zeros[:, 0:1])
+        idle_bank = psum.tile([P, BANK], F32, tag="bank")
+
+        def spin(count):
+            for i in range(count):
+                nc.tensor.matmul(out=idle_bank[:], lhsT=zeros[:, 0:P], rhs=zeros[:], start=True, stop=True)
+
+        spin(WARM_FIRST)
+
         x_rows = []
         for b in range(BATCHES):
             x_sb = keep.tile([P, HID], BF16, name="x_rows_%d" % b)
-            nc.sync.dma_start(out=x_sb[:], in_=hidden_states[b])
             x_rows.append(x_sb)
+        nc.sync.dma_start(out=x_rows[0][:, 0 : HID // 2], in_=hidden_states[0, :, 0 : HID // 2])
+        nc.sync.dma_start(out=x_rows[0][:, HID // 2 : HID], in_=hidden_states[0, :, HID // 2 : HID])
+        nc.sync.dma_start(out=x_rows[1][:], in_=hidden_states[1])
         cos_sb = keep.tile([P, P], BF16, name="cos_sb")
         sin_sb = keep.tile([P, P], BF16, name="sin_sb")
 
         w_scales = []
         w_words = []
-        first = 0
-        for c, width in enumerate(CHUNKS):
+
+        def load_chunk(c):
+            width = CHUNKS[c]
+            first = sum(CHUNKS[:c])
             scales = keep.tile([P, PASSES, width], U8, name="w_scales_%d" % c, align_bytes=64)
             nc.vector.memset(scales[:].bitcast(I32), 0)
             for r in range(4):
@@ -72,10 +90,12 @@ def tile_attention_pa_kernel(
                 .rearrange("g p c -> p g c"),
             )
             w_words.append(words)
-            first += width
-            if c == 0:
-                nc.sync.dma_start(out=cos_sb[:], in_=cos)
-                nc.sync.dma_start(out=sin_sb[:], in_=sin)
+
+        load_chunk(0)
+        nc.scalar.dma_start(out=cos_sb[:], in_=cos)
+        nc.scalar.dma_start(out=sin_sb[:], in_=sin)
+        load_chunk(1)
+        load_chunk(2)
 
         identity = keep.tile([P, P], F32, name="identity")
         make_identity(nc, identity[:])
@@ -93,6 +113,7 @@ def tile_attention_pa_kernel(
                             x_words[:, 256 * g + u : 256 * (g + 1) : 2],
                             identity[:],
                         )
+                spin(WARM_BETWEEN)
                 grouped = stage.tile([P, 2, P, 4], BF16, align_bytes=64)
                 copy_out = nc.vector.tensor_copy if half == 0 else nc.scalar.copy
                 copy_out(out=grouped[:].bitcast(F32), in_=turned[:].rearrange("p g u r -> p g r u"))
@@ -111,6 +132,9 @@ def tile_attention_pa_kernel(
         nc.vector.tensor_scalar_mul(out=factors[:, 1, :, 0], in0=sin_pairs[:, :, 0], scalar1=-1.0)
         nc.vector.tensor_copy(out=factors[:, 1, :, 1], in_=cos_pairs[:, :, 1])
         rotation_shape = [P, 2, HEADS_IN_BANK, PAIRS, 2]
+
+        for c in range(3, len(CHUNKS)):
+            load_chunk(c)
 
         results = {}
         first = 0

@@ -173,8 +173,7 @@ def tile_attention_pa_kernel(
                             in1=factors[:].unsqueeze(2).to_broadcast(rotation_shape),
                             op=MULT,
                         )
-                        adder = nc.vector if j == BANKS - 1 else nc.gpsimd
-                        adder.tensor_tensor(out=dest, in0=products[:, 0, :], in1=products[:, 1, :], op=ADD)
+                        nc.gpsimd.tensor_tensor(out=dest, in0=products[:, 0, :], in1=products[:, 1, :], op=ADD)
                     if (j + 1) % banks_in_store == 0:
                         j0 = j + 1 - banks_in_store
                         nc.sync.dma_start(

@@ -25,7 +25,8 @@ BANK = 512
 BANKS = FEATURES // BANK
 HEADS_IN_BANK = BANK // P
 PAIRS = P // 2
-CHUNKS = (512, 512, 1024, 1024, 1024, 1024, 1024)
+CHUNKS = ((0, 0, 512), (0, 512, 512), (1, 0, 1024), (2, 0, 1024), (0, 1024, 1024), (1, 1024, 1024), (2, 1024, 1024))
+PREFETCH = 3
 WARM_FIRST = 6
 WARM_BETWEEN = 1
 
@@ -68,34 +69,35 @@ def tile_attention_pa_kernel(
 
         w_scales = []
         w_words = []
-
-        def load_chunk(c):
-            width = CHUNKS[c]
-            first = sum(CHUNKS[:c])
+        for c, (part, start, width) in enumerate(CHUNKS):
             scales = keep.tile([P, PASSES, width], U8, name="w_scales_%d" % c, align_bytes=64)
             nc.vector.memset(scales[:].bitcast(I32), 0)
+            w_scales.append(scales)
+            words = keep.tile([P, PASSES, 2 * width], U8, name="w_words_%d" % c, align_bytes=64)
+            w_words.append(words)
+
+        def load_chunk(c):
+            part, start, width = CHUNKS[c]
+            first = part * FEATURES + start
             for r in range(4):
                 nc.sync.dma_start(
-                    out=scales[r : P : 32].bitcast(I32),
+                    out=w_scales[c][r : P : 32].bitcast(I32),
                     in_=w_qkv_scales[:, r : 16 : 4, first : first + width]
                     .bitcast(I32)
                     .rearrange("g j c -> j g c"),
                 )
-            w_scales.append(scales)
-            words = keep.tile([P, PASSES, 2 * width], U8, name="w_words_%d" % c, align_bytes=64)
             nc.sync.dma_start(
-                out=words[:].bitcast(I32),
+                out=w_words[c][:].bitcast(I32),
                 in_=w_qkv_words[:, :, 2 * first : 2 * (first + width)]
                 .bitcast(I32)
                 .rearrange("g p c -> p g c"),
             )
-            w_words.append(words)
 
         load_chunk(0)
-        nc.scalar.dma_start(out=cos_sb[:], in_=cos)
-        nc.scalar.dma_start(out=sin_sb[:], in_=sin)
-        load_chunk(1)
-        load_chunk(2)
+        nc.sync.dma_start(out=cos_sb[:], in_=cos)
+        nc.sync.dma_start(out=sin_sb[:], in_=sin)
+        for c in range(1, PREFETCH):
+            load_chunk(c)
 
         identity = keep.tile([P, P], F32, name="identity")
         make_identity(nc, identity[:])
@@ -115,8 +117,7 @@ def tile_attention_pa_kernel(
                         )
                 spin(WARM_BETWEEN)
                 grouped = stage.tile([P, 2, P, 4], BF16, align_bytes=64)
-                copy_out = nc.vector.tensor_copy if half == 0 else nc.scalar.copy
-                copy_out(out=grouped[:].bitcast(F32), in_=turned[:].rearrange("p g u r -> p g r u"))
+                nc.scalar.copy(out=grouped[:].bitcast(F32), in_=turned[:].rearrange("p g u r -> p g r u"))
                 passes = slice(2 * half, 2 * half + 2)
                 nc.vector.quantize_mx(
                     out=x_codes[:, b, passes, :].rearrange("p g r -> p (g r)").bitcast(FP8X4),
@@ -133,20 +134,14 @@ def tile_attention_pa_kernel(
         nc.vector.tensor_copy(out=factors[:, 1, :, 1], in_=cos_pairs[:, :, 1])
         rotation_shape = [P, 2, HEADS_IN_BANK, PAIRS, 2]
 
-        for c in range(3, len(CHUNKS)):
-            load_chunk(c)
-
-        results = {}
-        first = 0
-        for c, width in enumerate(CHUNKS):
-            part = first // FEATURES
-            banks_in_store = 1 if part == V_PART else 2
+        for c, (part, start, width) in enumerate(CHUNKS):
+            if c + PREFETCH < len(CHUNKS):
+                load_chunk(c + PREFETCH)
+            last_chunk = c == len(CHUNKS) - 1
             for b in range(BATCHES):
-                if (part, b) not in results:
-                    results[(part, b)] = keep.tile([P, FEATURES], F32, name="result_%d_%d" % (part, b))
-                result = results[(part, b)]
+                result = keep.tile([P, width], F32, name="result_%d_%d" % (c, b))
+                banks_in_store = 1 if (last_chunk and b == BATCHES - 1) else width // BANK
                 for i in range(width // BANK):
-                    j = (first % FEATURES) // BANK + i
                     at = BANK * i
                     acc = psum.tile([P, BANK], F32, tag="bank")
                     for g in range(PASSES):
@@ -159,7 +154,7 @@ def tile_attention_pa_kernel(
                             start=(g == 0),
                             stop=(g == PASSES - 1),
                         )
-                    dest = result[:, BANK * j : BANK * (j + 1)]
+                    dest = result[:, at : at + BANK]
                     if part == V_PART:
                         nc.scalar.copy(out=dest, in_=acc[:])
                     else:
@@ -174,12 +169,12 @@ def tile_attention_pa_kernel(
                             op=MULT,
                         )
                         nc.gpsimd.tensor_tensor(out=dest, in0=products[:, 0, :], in1=products[:, 1, :], op=ADD)
-                    if (j + 1) % banks_in_store == 0:
-                        j0 = j + 1 - banks_in_store
+                    if (i + 1) % banks_in_store == 0:
+                        i0 = i + 1 - banks_in_store
+                        head0 = (start + BANK * i0) // P
                         nc.sync.dma_start(
-                            out=outs[part][b, :, HEADS_IN_BANK * j0 : HEADS_IN_BANK * (j + 1), :].rearrange(
+                            out=outs[part][b, :, head0 : head0 + HEADS_IN_BANK * banks_in_store, :].rearrange(
                                 "s h d -> s (h d)"
                             ),
-                            in_=result[:, BANK * j0 : BANK * (j + 1)],
+                            in_=result[:, BANK * i0 : BANK * (i + 1)],
                         )
-            first += width

@@ -25,8 +25,7 @@ BANK = 512
 BANKS = FEATURES // BANK
 HEADS_IN_BANK = BANK // P
 PAIRS = P // 2
-CHUNKS = ((0, 0, 512), (0, 512, 512), (1, 0, 1024), (2, 0, 1024), (0, 1024, 1024), (1, 1024, 1024), (2, 1024, 1024))
-PREFETCH = 3
+CHUNKS = ((0, 0, 1024), (0, 1024, 1024), (1, 0, 1024), (1, 1024, 1024), (2, 0, 2048))
 WARM_FIRST = 6
 WARM_BETWEEN = 1
 
@@ -68,36 +67,32 @@ def tile_attention_pa_kernel(
         sin_sb = keep.tile([P, P], BF16, name="sin_sb")
 
         w_scales = []
-        w_words = []
-        for c, (part, start, width) in enumerate(CHUNKS):
-            scales = keep.tile([P, PASSES, width], U8, name="w_scales_%d" % c, align_bytes=64)
+        for part in range(PARTS):
+            scales = keep.tile([P, PASSES, FEATURES], U8, name="w_scales_%d" % part, align_bytes=64)
             nc.vector.memset(scales[:].bitcast(I32), 0)
             w_scales.append(scales)
-            words = keep.tile([P, PASSES, 2 * width], U8, name="w_words_%d" % c, align_bytes=64)
-            w_words.append(words)
-
-        def load_chunk(c):
-            part, start, width = CHUNKS[c]
+        w_words = []
+        for c, (part, start, width) in enumerate(CHUNKS):
+            if start == 0:
+                for q in range(8):
+                    nc.sync.dma_start(
+                        out=w_scales[part][32 * (q // 4) + q % 4 : P : 64].bitcast(I32),
+                        in_=w_qkv_scales[:, q : 16 : 8, part * FEATURES : (part + 1) * FEATURES]
+                        .bitcast(I32)
+                        .rearrange("g j c -> j g c"),
+                    )
             first = part * FEATURES + start
-            for r in range(4):
-                nc.sync.dma_start(
-                    out=w_scales[c][r : P : 32].bitcast(I32),
-                    in_=w_qkv_scales[:, r : 16 : 4, first : first + width]
-                    .bitcast(I32)
-                    .rearrange("g j c -> j g c"),
-                )
+            words = keep.tile([P, PASSES, 2 * width], U8, name="w_words_%d" % c, align_bytes=64)
             nc.sync.dma_start(
-                out=w_words[c][:].bitcast(I32),
+                out=words[:].bitcast(I32),
                 in_=w_qkv_words[:, :, 2 * first : 2 * (first + width)]
                 .bitcast(I32)
                 .rearrange("g p c -> p g c"),
             )
-
-        load_chunk(0)
-        nc.sync.dma_start(out=cos_sb[:], in_=cos)
-        nc.sync.dma_start(out=sin_sb[:], in_=sin)
-        for c in range(1, PREFETCH):
-            load_chunk(c)
+            w_words.append(words)
+            if c == 0:
+                nc.sync.dma_start(out=cos_sb[:], in_=cos)
+                nc.sync.dma_start(out=sin_sb[:], in_=sin)
 
         identity = keep.tile([P, P], F32, name="identity")
         make_identity(nc, identity[:])
@@ -134,15 +129,17 @@ def tile_attention_pa_kernel(
         nc.vector.tensor_copy(out=factors[:, 1, :, 1], in_=cos_pairs[:, :, 1])
         rotation_shape = [P, 2, HEADS_IN_BANK, PAIRS, 2]
 
+        results = {}
         for c, (part, start, width) in enumerate(CHUNKS):
-            if c + PREFETCH < len(CHUNKS):
-                load_chunk(c + PREFETCH)
-            last_chunk = c == len(CHUNKS) - 1
             for b in range(BATCHES):
-                result = keep.tile([P, width], F32, name="result_%d_%d" % (c, b))
-                banks_in_store = 1 if (last_chunk and b == BATCHES - 1) else width // BANK
+                if (part, b) not in results:
+                    results[(part, b)] = keep.tile([P, FEATURES], F32, name="result_%d_%d" % (part, b))
+                result = results[(part, b)]
+                final = c == len(CHUNKS) - 1 and b == BATCHES - 1
+                store_after = {1: 0, 2: 2, 3: 3} if final else {BANKS - 1: 0}
                 for i in range(width // BANK):
                     at = BANK * i
+                    j = start // BANK + i
                     acc = psum.tile([P, BANK], F32, tag="bank")
                     for g in range(PASSES):
                         nc.tensor.matmul_mx(
@@ -150,11 +147,11 @@ def tile_attention_pa_kernel(
                             lhsT=x_codes[:, b, g, :].bitcast(FP8X4),
                             lhsT_scale=x_scales[:, b, g, :],
                             rhs=w_words[c][:, g, 2 * at : 2 * (at + BANK)].bitcast(FP4X4),
-                            rhs_scale=w_scales[c][:, g, at : at + BANK],
+                            rhs_scale=w_scales[part][:, g, BANK * j : BANK * (j + 1)],
                             start=(g == 0),
                             stop=(g == PASSES - 1),
                         )
-                    dest = result[:, at : at + BANK]
+                    dest = result[:, BANK * j : BANK * (j + 1)]
                     if part == V_PART:
                         nc.scalar.copy(out=dest, in_=acc[:])
                     else:
@@ -169,12 +166,11 @@ def tile_attention_pa_kernel(
                             op=MULT,
                         )
                         nc.gpsimd.tensor_tensor(out=dest, in0=products[:, 0, :], in1=products[:, 1, :], op=ADD)
-                    if (i + 1) % banks_in_store == 0:
-                        i0 = i + 1 - banks_in_store
-                        head0 = (start + BANK * i0) // P
+                    if j in store_after:
+                        j0 = store_after[j]
                         nc.sync.dma_start(
-                            out=outs[part][b, :, head0 : head0 + HEADS_IN_BANK * banks_in_store, :].rearrange(
+                            out=outs[part][b, :, HEADS_IN_BANK * j0 : HEADS_IN_BANK * (j + 1), :].rearrange(
                                 "s h d -> s (h d)"
                             ),
-                            in_=result[:, BANK * i0 : BANK * (i + 1)],
+                            in_=result[:, BANK * j0 : BANK * (j + 1)],
                         )

@@ -71,16 +71,21 @@ def tile_attention_pa_kernel(
             scales = keep.tile([P, PASSES, FEATURES], U8, name="w_scales_%d" % part, align_bytes=64)
             nc.vector.memset(scales[:].bitcast(I32), 0)
             w_scales.append(scales)
+
+        def load_scales(part):
+            count = 8 if part == 0 else 4
+            for q in range(count):
+                nc.sync.dma_start(
+                    out=w_scales[part][32 * (q // 4) + q % 4 : P : 8 * count].bitcast(I32),
+                    in_=w_qkv_scales[:, q : 16 : count, part * FEATURES : (part + 1) * FEATURES]
+                    .bitcast(I32)
+                    .rearrange("g j c -> j g c"),
+                )
+
         w_words = []
         for c, (part, start, width) in enumerate(CHUNKS):
-            if start == 0:
-                for q in range(8):
-                    nc.sync.dma_start(
-                        out=w_scales[part][32 * (q // 4) + q % 4 : P : 64].bitcast(I32),
-                        in_=w_qkv_scales[:, q : 16 : 8, part * FEATURES : (part + 1) * FEATURES]
-                        .bitcast(I32)
-                        .rearrange("g j c -> j g c"),
-                    )
+            if start == 0 and part != V_PART:
+                load_scales(part)
             first = part * FEATURES + start
             words = keep.tile([P, PASSES, 2 * width], U8, name="w_words_%d" % c, align_bytes=64)
             nc.sync.dma_start(
@@ -90,6 +95,8 @@ def tile_attention_pa_kernel(
                 .rearrange("g p c -> p g c"),
             )
             w_words.append(words)
+            if part == V_PART:
+                load_scales(part)
             if c == 0:
                 nc.sync.dma_start(out=cos_sb[:], in_=cos)
                 nc.sync.dma_start(out=sin_sb[:], in_=sin)

@@ -25,7 +25,7 @@ BANK = 512
 BANKS = FEATURES // BANK
 HEADS_IN_BANK = BANK // P
 PAIRS = P // 2
-CHUNKS = ((0, 0, 1024), (0, 1024, 1024), (1, 0, 1024), (1, 1024, 1024), (2, 0, 2048))
+CHUNKS = ((0, 0, 512), (0, 512, 512), (0, 1024, 1024), (1, 0, 1024), (1, 1024, 1024), (2, 0, 2048))
 WARM_FIRST = 6
 WARM_BETWEEN = 1
 
@@ -60,9 +60,8 @@ def tile_attention_pa_kernel(
         for b in range(BATCHES):
             x_sb = keep.tile([P, HID], BF16, name="x_rows_%d" % b)
             x_rows.append(x_sb)
-        nc.sync.dma_start(out=x_rows[0][:, 0 : HID // 2], in_=hidden_states[0, :, 0 : HID // 2])
-        nc.sync.dma_start(out=x_rows[0][:, HID // 2 : HID], in_=hidden_states[0, :, HID // 2 : HID])
-        nc.sync.dma_start(out=x_rows[1][:], in_=hidden_states[1])
+        for b in range(BATCHES):
+            nc.sync.dma_start(out=x_rows[b][:], in_=hidden_states[b])
         cos_sb = keep.tile([P, P], BF16, name="cos_sb")
         sin_sb = keep.tile([P, P], BF16, name="sin_sb")
 
@@ -73,11 +72,10 @@ def tile_attention_pa_kernel(
             w_scales.append(scales)
 
         def load_scales(part):
-            count = 8 if part == 0 else 4
-            for q in range(count):
+            for q in range(4):
                 nc.sync.dma_start(
-                    out=w_scales[part][32 * (q // 4) + q % 4 : P : 8 * count].bitcast(I32),
-                    in_=w_qkv_scales[:, q : 16 : count, part * FEATURES : (part + 1) * FEATURES]
+                    out=w_scales[part][q : P : 32].bitcast(I32),
+                    in_=w_qkv_scales[:, q : 16 : 4, part * FEATURES : (part + 1) * FEATURES]
                     .bitcast(I32)
                     .rearrange("g j c -> j g c"),
                 )

@@ -26,6 +26,10 @@ BANKS = FEATURES // BANK
 HEADS_IN_BANK = BANK // P
 PAIRS = P // 2
 CHUNKS = ((0, 0, 512), (0, 512, 512), (0, 1024, 1024), (1, 0, 1024), (1, 1024, 1024), (2, 0, 2048))
+ROUNDS = (
+    (0, 0, 0, 1), (0, 1, 0, 1), (0, 0, 1, 1), (0, 1, 1, 1), (0, 0, 2, 2), (0, 1, 2, 2),
+    (1, 0, 0, 4), (1, 1, 0, 4), (2, 0, 0, 4), (2, 1, 0, 4),
+)
 WARM_FIRST = 6
 WARM_BETWEEN = 1
 
@@ -72,15 +76,16 @@ def tile_attention_pa_kernel(
             w_scales.append(scales)
 
         def load_scales(part):
-            for q in range(4):
+            count = 4 if part == V_PART else 8
+            for q in range(count):
                 nc.sync.dma_start(
-                    out=w_scales[part][q : P : 32].bitcast(I32),
-                    in_=w_qkv_scales[:, q : 16 : 4, part * FEATURES : (part + 1) * FEATURES]
+                    out=w_scales[part][32 * (q // 4) + q % 4 : P : 8 * count].bitcast(I32),
+                    in_=w_qkv_scales[:, q : 16 : count, part * FEATURES : (part + 1) * FEATURES]
                     .bitcast(I32)
                     .rearrange("g j c -> j g c"),
                 )
 
-        w_words = []
+        w_words = {}
         for c, (part, start, width) in enumerate(CHUNKS):
             if start == 0 and part != V_PART:
                 load_scales(part)
@@ -92,7 +97,8 @@ def tile_attention_pa_kernel(
                 .bitcast(I32)
                 .rearrange("g p c -> p g c"),
             )
-            w_words.append(words)
+            for i in range(width // BANK):
+                w_words[(part, start // BANK + i)] = words[:, :, 2 * BANK * i : 2 * BANK * (i + 1)]
             if part == V_PART:
                 load_scales(part)
             if c == 0:
@@ -134,48 +140,55 @@ def tile_attention_pa_kernel(
         nc.vector.tensor_copy(out=factors[:, 1, :, 1], in_=cos_pairs[:, :, 1])
         rotation_shape = [P, 2, HEADS_IN_BANK, PAIRS, 2]
 
+        def add_products(engine, dest, products):
+            engine.tensor_tensor(out=dest, in0=products[:, 0, :], in1=products[:, 1, :], op=ADD)
+
         results = {}
-        for c, (part, start, width) in enumerate(CHUNKS):
-            for b in range(BATCHES):
-                if (part, b) not in results:
-                    results[(part, b)] = keep.tile([P, FEATURES], F32, name="result_%d_%d" % (part, b))
-                result = results[(part, b)]
-                final = c == len(CHUNKS) - 1 and b == BATCHES - 1
-                store_after = {1: 0, 2: 2, 3: 3} if final else {BANKS - 1: 0}
-                for i in range(width // BANK):
-                    at = BANK * i
-                    j = start // BANK + i
-                    acc = psum.tile([P, BANK], F32, tag="bank")
-                    for g in range(PASSES):
-                        nc.tensor.matmul_mx(
-                            out=acc[:],
-                            lhsT=x_codes[:, b, g, :].bitcast(FP8X4),
-                            lhsT_scale=x_scales[:, b, g, :],
-                            rhs=w_words[c][:, g, 2 * at : 2 * (at + BANK)].bitcast(FP4X4),
-                            rhs_scale=w_scales[part][:, g, BANK * j : BANK * (j + 1)],
-                            start=(g == 0),
-                            stop=(g == PASSES - 1),
-                        )
-                    dest = result[:, BANK * j : BANK * (j + 1)]
-                    if part == V_PART:
-                        nc.scalar.copy(out=dest, in_=acc[:])
+        for part, b, first_bank, banks in ROUNDS:
+            if (part, b) not in results:
+                results[(part, b)] = keep.tile([P, FEATURES], F32, name="result_%d_%d" % (part, b))
+            result = results[(part, b)]
+            final = part == V_PART and b == BATCHES - 1
+            store_after = {1: 0, 2: 2, 3: 3} if final else {BANKS - 1: 0}
+            late = []
+            for j in range(first_bank, first_bank + banks):
+                acc = psum.tile([P, BANK], F32, tag="bank")
+                for g in range(PASSES):
+                    nc.tensor.matmul_mx(
+                        out=acc[:],
+                        lhsT=x_codes[:, b, g, :].bitcast(FP8X4),
+                        lhsT_scale=x_scales[:, b, g, :],
+                        rhs=w_words[(part, j)][:, g, :].bitcast(FP4X4),
+                        rhs_scale=w_scales[part][:, g, BANK * j : BANK * (j + 1)],
+                        start=(g == 0),
+                        stop=(g == PASSES - 1),
+                    )
+                dest = result[:, BANK * j : BANK * (j + 1)]
+                if part == V_PART:
+                    nc.scalar.copy(out=dest, in_=acc[:])
+                else:
+                    products = stage.tile([P, 2, BANK], F32)
+                    nc.vector.tensor_tensor(
+                        out=products[:].rearrange("p e (h i t) -> p e h i t", i=PAIRS, t=2),
+                        in0=acc[:]
+                        .rearrange("p (h i e) -> p e h i", i=PAIRS, e=2)
+                        .unsqueeze(4)
+                        .to_broadcast(rotation_shape),
+                        in1=factors[:].unsqueeze(2).to_broadcast(rotation_shape),
+                        op=MULT,
+                    )
+                    if part == V_PART - 1 and b == BATCHES - 1 and j >= BANKS - 2:
+                        late.append((dest, products))
                     else:
-                        products = stage.tile([P, 2, BANK], F32)
-                        nc.vector.tensor_tensor(
-                            out=products[:].rearrange("p e (h i t) -> p e h i t", i=PAIRS, t=2),
-                            in0=acc[:]
-                            .rearrange("p (h i e) -> p e h i", i=PAIRS, e=2)
-                            .unsqueeze(4)
-                            .to_broadcast(rotation_shape),
-                            in1=factors[:].unsqueeze(2).to_broadcast(rotation_shape),
-                            op=MULT,
-                        )
-                        nc.gpsimd.tensor_tensor(out=dest, in0=products[:, 0, :], in1=products[:, 1, :], op=ADD)
-                    if j in store_after:
-                        j0 = store_after[j]
-                        nc.sync.dma_start(
-                            out=outs[part][b, :, HEADS_IN_BANK * j0 : HEADS_IN_BANK * (j + 1), :].rearrange(
-                                "s h d -> s (h d)"
-                            ),
-                            in_=result[:, BANK * j0 : BANK * (j + 1)],
-                        )
+                        add_products(nc.gpsimd, dest, products)
+                if j == BANKS - 1:
+                    for dest, products in late:
+                        add_products(nc.vector, dest, products)
+                if j in store_after:
+                    j0 = store_after[j]
+                    nc.sync.dma_start(
+                        out=outs[part][b, :, HEADS_IN_BANK * j0 : HEADS_IN_BANK * (j + 1), :].rearrange(
+                            "s h d -> s (h d)"
+                        ),
+                        in_=result[:, BANK * j0 : BANK * (j + 1)],
+                    )

@@ -62,16 +62,16 @@ def tile_attention_pa_kernel(
 
         x_rows = []
         for b in range(BATCHES):
-            x_sb = keep.tile([P, HID], BF16, name="x_rows_%d" % b)
+            x_sb = keep.tile([P, HID], BF16, name="x_rows_%d" % b, align_bytes=256)
             x_rows.append(x_sb)
         for b in range(BATCHES):
             nc.sync.dma_start(out=x_rows[b][:], in_=hidden_states[b])
-        cos_sb = keep.tile([P, P], BF16, name="cos_sb")
-        sin_sb = keep.tile([P, P], BF16, name="sin_sb")
+        cos_sb = keep.tile([P, P], BF16, name="cos_sb", align_bytes=256)
+        sin_sb = keep.tile([P, P], BF16, name="sin_sb", align_bytes=256)
 
         w_scales = []
         for part in range(PARTS):
-            scales = keep.tile([P, PASSES, FEATURES], U8, name="w_scales_%d" % part, align_bytes=64)
+            scales = keep.tile([P, PASSES, FEATURES], U8, name="w_scales_%d" % part, align_bytes=256)
             nc.vector.memset(scales[:].bitcast(I32), 0)
             w_scales.append(scales)
 
@@ -90,7 +90,7 @@ def tile_attention_pa_kernel(
             if start == 0 and part != V_PART:
                 load_scales(part)
             first = part * FEATURES + start
-            words = keep.tile([P, PASSES, 2 * width], U8, name="w_words_%d" % c, align_bytes=64)
+            words = keep.tile([P, PASSES, 2 * width], U8, name="w_words_%d" % c, align_bytes=256)
             nc.sync.dma_start(
                 out=words[:].bitcast(I32),
                 in_=w_qkv_words[:, :, 2 * first : 2 * (first + width)]
@@ -107,8 +107,8 @@ def tile_attention_pa_kernel(
 
         identity = keep.tile([P, P], F32, name="identity")
         make_identity(nc, identity[:])
-        x_codes = keep.tile([P, BATCHES, PASSES, P], U32, name="x_codes", align_bytes=64)
-        x_scales = keep.tile([P, BATCHES, PASSES, P], U8, name="x_scales", align_bytes=64)
+        x_codes = keep.tile([P, BATCHES, PASSES, P], U32, name="x_codes", align_bytes=256)
+        x_scales = keep.tile([P, BATCHES, PASSES, P], U8, name="x_scales", align_bytes=256)
         for b in range(BATCHES):
             x_words = x_rows[b][:].bitcast(F32)
             for half in range(PASSES // 2):
@@ -122,7 +122,7 @@ def tile_attention_pa_kernel(
                             identity[:],
                         )
                 spin(WARM_BETWEEN)
-                grouped = stage.tile([P, 2, P, 4], BF16, align_bytes=64)
+                grouped = stage.tile([P, 2, P, 4], BF16, align_bytes=256)
                 nc.scalar.copy(out=grouped[:].bitcast(F32), in_=turned[:].rearrange("p g u r -> p g r u"))
                 passes = slice(2 * half, 2 * half + 2)
                 nc.vector.quantize_mx(
@@ -146,7 +146,7 @@ def tile_attention_pa_kernel(
         results = {}
         for part, b, first_bank, banks in ROUNDS:
             if (part, b) not in results:
-                results[(part, b)] = keep.tile([P, FEATURES], F32, name="result_%d_%d" % (part, b))
+                results[(part, b)] = keep.tile([P, FEATURES], F32, name="result_%d_%d" % (part, b), align_bytes=256)
             result = results[(part, b)]
             final = part == V_PART and b == BATCHES - 1
             store_after = {1: 0, 2: 2, 3: 3} if final else {BANKS - 1: 0}

from contextlib import ExitStack

import concourse.mybir as mybir
from concourse.masks import make_identity

F32 = mybir.dt.float32
BF16 = mybir.dt.bfloat16
I32 = mybir.dt.int32
U32 = mybir.dt.uint32
U8 = mybir.dt.uint8
FP8X4 = mybir.dt.float8_e4m3fn_x4
FP4X4 = mybir.dt.float4_e2m1fn_x4
MULT = mybir.AluOpType.mult
ADD = mybir.AluOpType.add

P = 128
BATCHES = 2
HID = 2048
K_PASS = 4 * P
PASSES = HID // K_PASS
PARTS = 3
V_PART = 2
FEATURES = 2048
BANK = 512
BANKS = FEATURES // BANK
HEADS_IN_BANK = BANK // P
PAIRS = P // 2
CHUNKS = ((0, 0, 512), (0, 512, 512), (0, 1024, 1024), (1, 0, 1024), (1, 1024, 1024), (2, 0, 2048))
ROUNDS = (
    (0, 0, 0, 1), (0, 1, 0, 1), (0, 0, 1, 1), (0, 1, 1, 1), (0, 0, 2, 2), (0, 1, 2, 2),
    (1, 0, 0, 4), (1, 1, 0, 4), (2, 0, 0, 4), (2, 1, 0, 4),
)
WARM_FIRST = 6
WARM_BETWEEN = 1

FLOPS = 2 * BATCHES * P * HID * PARTS * FEATURES


def tile_attention_pa_kernel(
    tc, hidden_states, cos, sin, w_qkv_words, w_qkv_scales, out_0, out_1, out_2
):
    nc = tc.nc
    outs = (out_0, out_1, out_2)

    with ExitStack() as stack:
        stack.enter_context(tc.manual_schedule())
        keep = stack.enter_context(tc.tile_pool(name="keep", bufs=1))
        stage = stack.enter_context(tc.tile_pool(name="stage", bufs=4))
        psum = stack.enter_context(tc.psum_pool(name="psum", bufs=8))

        zeros = keep.tile([P, BANK], BF16, name="zeros")
        nc.vector.memset(zeros[:], 0.0)
        table_warm = keep.tile([P, 1], BF16, name="table_warm")
        nc.scalar.copy(out=table_warm[:], in_=zeros[:, 0:1])
        idle_bank = psum.tile([P, BANK], F32, tag="bank")

        def spin(count):
            for i in range(count):
                nc.tensor.matmul(out=idle_bank[:], lhsT=zeros[:, 0:P], rhs=zeros[:], start=True, stop=True)

        spin(WARM_FIRST)

        x_rows = []
        for b in range(BATCHES):
            x_sb = keep.tile([P, HID], BF16, name="x_rows_%d" % b, align_bytes=256)
            x_rows.append(x_sb)
        for b in range(BATCHES):
            nc.sync.dma_start(out=x_rows[b][:], in_=hidden_states[b])
        cos_sb = keep.tile([P, P], BF16, name="cos_sb", align_bytes=256)
        sin_sb = keep.tile([P, P], BF16, name="sin_sb", align_bytes=256)

        w_scales = []
        for part in range(PARTS):
            scales = keep.tile([P, PASSES, FEATURES], U8, name="w_scales_%d" % part, align_bytes=256)
            nc.vector.memset(scales[:].bitcast(I32), 0)
            w_scales.append(scales)

        def load_scales(part):
            count = 4 if part == V_PART else 8
            for q in range(count):
                nc.sync.dma_start(
                    out=w_scales[part][32 * (q // 4) + q % 4 : P : 8 * count].bitcast(I32),
                    in_=w_qkv_scales[:, q : 16 : count, part * FEATURES : (part + 1) * FEATURES]
                    .bitcast(I32)
                    .rearrange("g j c -> j g c"),
                )

        w_words = {}
        for c, (part, start, width) in enumerate(CHUNKS):
            if start == 0 and part != V_PART:
                load_scales(part)
            first = part * FEATURES + start
            words = keep.tile([P, PASSES, 2 * width], U8, name="w_words_%d" % c, align_bytes=256)
            nc.sync.dma_start(
                out=words[:].bitcast(I32),
                in_=w_qkv_words[:, :, 2 * first : 2 * (first + width)]
                .bitcast(I32)
                .rearrange("g p c -> p g c"),
            )
            for i in range(width // BANK):
                w_words[(part, start // BANK + i)] = words[:, :, 2 * BANK * i : 2 * BANK * (i + 1)]
            if part == V_PART:
                load_scales(part)
            if c == 0:
                nc.sync.dma_start(out=cos_sb[:], in_=cos)
                nc.sync.dma_start(out=sin_sb[:], in_=sin)

        identity = keep.tile([P, P], F32, name="identity")
        make_identity(nc, identity[:])
        x_codes = keep.tile([P, BATCHES, PASSES, P], U32, name="x_codes", align_bytes=256)
        x_scales = keep.tile([P, BATCHES, PASSES, P], U8, name="x_scales", align_bytes=256)
        for b in range(BATCHES):
            x_words = x_rows[b][:].bitcast(F32)
            for half in range(PASSES // 2):
                turned = psum.tile([P, 2, 2, P], F32, tag="bank")
                for gi in range(2):
                    g = 2 * half + gi
                    for u in range(2):
                        nc.tensor.transpose(
                            turned[:, gi, u, :],
                            x_words[:, 256 * g + u : 256 * (g + 1) : 2],
                            identity[:],
                        )
                spin(WARM_BETWEEN)
                grouped = stage.tile([P, 2, P, 4], BF16, align_bytes=256)
                nc.scalar.copy(out=grouped[:].bitcast(F32), in_=turned[:].rearrange("p g u r -> p g r u"))
                passes = slice(2 * half, 2 * half + 2)
                nc.vector.quantize_mx(
                    out=x_codes[:, b, passes, :].rearrange("p g r -> p (g r)").bitcast(FP8X4),
                    scales=x_scales[:, b, passes, :].rearrange("p g r -> p (g r)"),
                    in_=grouped[:].rearrange("p g r t -> p (g r t)"),
                )

        cos_pairs = cos_sb[:].rearrange("p (i t) -> p i t", t=2)
        sin_pairs = sin_sb[:].rearrange("p (i t) -> p i t", t=2)
        factors = keep.tile([P, 2, PAIRS, 2], F32, name="factors")
        nc.vector.tensor_copy(out=factors[:, 0, :, 0], in_=cos_pairs[:, :, 0])
        nc.vector.tensor_copy(out=factors[:, 0, :, 1], in_=sin_pairs[:, :, 1])
        nc.vector.tensor_scalar_mul(out=factors[:, 1, :, 0], in0=sin_pairs[:, :, 0], scalar1=-1.0)
        nc.vector.tensor_copy(out=factors[:, 1, :, 1], in_=cos_pairs[:, :, 1])
        rotation_shape = [P, 2, HEADS_IN_BANK, PAIRS, 2]

        def add_products(engine, dest, products):
            engine.tensor_tensor(out=dest, in0=products[:, 0, :], in1=products[:, 1, :], op=ADD)

        results = {}
        for part, b, first_bank, banks in ROUNDS:
            if (part, b) not in results:
                results[(part, b)] = keep.tile([P, FEATURES], F32, name="result_%d_%d" % (part, b), align_bytes=256)
            result = results[(part, b)]
            final = part == V_PART and b == BATCHES - 1
            store_after = {1: 0, 2: 2, 3: 3} if final else {BANKS - 1: 0}
            late = []
            for j in range(first_bank, first_bank + banks):
                acc = psum.tile([P, BANK], F32, tag="bank")
                for g in range(PASSES):
                    nc.tensor.matmul_mx(
                        out=acc[:],
                        lhsT=x_codes[:, b, g, :].bitcast(FP8X4),
                        lhsT_scale=x_scales[:, b, g, :],
                        rhs=w_words[(part, j)][:, g, :].bitcast(FP4X4),
                        rhs_scale=w_scales[part][:, g, BANK * j : BANK * (j + 1)],
                        start=(g == 0),
                        stop=(g == PASSES - 1),
                    )
                dest = result[:, BANK * j : BANK * (j + 1)]
                if part == V_PART:
                    nc.scalar.copy(out=dest, in_=acc[:])
                else:
                    products = stage.tile([P, 2, BANK], F32)
                    nc.vector.tensor_tensor(
                        out=products[:].rearrange("p e (h i t) -> p e h i t", i=PAIRS, t=2),
                        in0=acc[:]
                        .rearrange("p (h i e) -> p e h i", i=PAIRS, e=2)
                        .unsqueeze(4)
                        .to_broadcast(rotation_shape),
                        in1=factors[:].unsqueeze(2).to_broadcast(rotation_shape),
                        op=MULT,
                    )
                    if part == V_PART - 1 and b == BATCHES - 1 and j >= BANKS - 2:
                        late.append((dest, products))
                    else:
                        add_products(nc.gpsimd, dest, products)
                if j == BANKS - 1:
                    for dest, products in late:
                        add_products(nc.vector, dest, products)
                if j in store_after:
                    j0 = store_after[j]
                    nc.sync.dma_start(
                        out=outs[part][b, :, HEADS_IN_BANK * j0 : HEADS_IN_BANK * (j + 1), :].rearrange(
                            "s h d -> s (h d)"
                        ),
                        in_=result[:, BANK * j0 : BANK * (j + 1)],
                    )
